import numpy as np
import ml_dtypes


def mxq(x, axis, fmt="e4m3"):
    dtype, down = {"e4m3": (ml_dtypes.float8_e4m3fn, 7), "e5m2": (ml_dtypes.float8_e5m2, 14)}[fmt]
    v = np.moveaxis(np.asarray(x, np.float32).astype(ml_dtypes.bfloat16).astype(np.float64), axis, -1)
    blocks = v.reshape(v.shape[:-1] + (-1, 32))
    amax = np.abs(blocks).max(-1, keepdims=True)
    byte = np.maximum(np.where(amax > 0, np.frexp(amax)[1] - 1 + 127, 0) - down, 1)
    scale = np.exp2(byte - 127.0)
    codes = (blocks / scale).astype(np.float32).astype(dtype).astype(np.float64)
    return np.moveaxis((codes * scale).reshape(v.shape), -1, axis)


WIDE = False


def mx_kscale(k):
    if not WIDE:
        return np.ones(k)
    levels = np.array([10, -10, 5, -5, 0])
    a = np.random.permutation(np.resize(levels, k // 512 * 4)).reshape(k // 512, 4)
    idx = np.arange(k)
    return np.exp2(a[idx // 512, idx % 128 // 32])


BF16 = ml_dtypes.bfloat16


def bf(x):
    return np.asarray(x, np.float32).astype(BF16)


def f64(x):
    return np.asarray(x).astype(np.float64)


B, N, D, H, DH, WS = 4, 1024, 1024, 4, 128, 512
INNER = H * DH
NW = N // WS
BW = B * NW


def elu(u):
    return np.where(u > 0.0, u, np.exp(np.minimum(u, 0.0)) - 1.0)


def heads(t):
    return t.reshape(BW, WS, H, DH).transpose(0, 2, 1, 3)


def setup_inputs():
    s = mx_kscale(D)
    return {"x": bf(np.random.standard_normal((B, N, D)) * s),
            "w_k": bf(np.random.standard_normal((D, INNER)) / np.sqrt(D) / s[:, None]),
            "w_v": bf(np.random.standard_normal((D, INNER)) * 0.3 / np.sqrt(D * WS) / s[:, None])}


def reference(x, w_k, w_v):
    xq = mxq(f64(x).reshape(BW, WS, D), 2, "e4m3")
    k = heads(xq @ mxq(f64(w_k), 0, "e4m3"))
    v = heads(xq @ mxq(f64(w_v), 0, "e4m3"))
    kf = elu(k) + 1.0
    return mxq(kf, 2, "e4m3").transpose(0, 1, 3, 2) @ mxq(v, 2, "e4m3")

@@ -1,0 +1,173 @@
+from contextlib import ExitStack
+
+import concourse.mybir as mybir
+from concourse.masks import make_identity
+
+F32 = mybir.dt.float32
+BF16 = mybir.dt.bfloat16
+U32 = mybir.dt.uint32
+U8 = mybir.dt.uint8
+FP8X4 = mybir.dt.float8_e4m3fn_x4
+ACT = mybir.ActivationFunctionType
+ALU = mybir.AluOpType
+
+P = 128
+PACK = 4
+K_PASS = P * PACK
+WINDOWS = 8
+TOKENS = 512
+FEATURES = 1024
+PASSES = FEATURES // K_PASS
+HEADS = 4
+DH = 128
+INNER = HEADS * DH
+PAIRS = 2
+
+FLOPS = 2 * WINDOWS * TOKENS * FEATURES * 2 * INNER + 2 * WINDOWS * HEADS * TOKENS * DH * DH
+
+
+def tile_localcontextprocessor_pa_t_kernel(tc, x, w_k, w_v, out):
+    nc = tc.nc
+    with ExitStack() as ctx:
+        const = ctx.enter_context(tc.tile_pool(name="const", bufs=1))
+        rows = ctx.enter_context(tc.tile_pool(name="rows", bufs=WINDOWS))
+        stage = ctx.enter_context(tc.tile_pool(name="stage", bufs=2))
+        exps = ctx.enter_context(tc.tile_pool(name="exps", bufs=4))
+        psum = ctx.enter_context(tc.psum_pool(name="psum", bufs=8))
+
+        x_windows = x.rearrange("b (n p j) d -> (b n) p (j d)", n=2, p=P, j=PACK)
+
+        def load_window(w):
+            x_rows = rows.tile([P, PACK * FEATURES], BF16, name="x_rows")
+            nc.sync.dma_start(out=x_rows[:], in_=x_windows[w])
+            return x_rows
+
+        def load_weight(w_dram, name):
+            w_raw = const.tile([P, PASSES * PACK * INNER], BF16, name=name)
+            nc.sync.dma_start(
+                out=w_raw[:].rearrange("q (s r) -> q s r", s=PASSES * PAIRS),
+                in_=w_dram.rearrange("(s q e) c -> q s (e c)", s=PASSES * PAIRS, q=P, e=2),
+            )
+            return w_raw
+
+        wk_raw = load_weight(w_k, "wk_raw")
+        x_tiles = [load_window(0)]
+        wv_raw = load_weight(w_v, "wv_raw")
+        for w in range(1, WINDOWS):
+            x_tiles.append(load_window(w))
+
+        ident = const.tile([P, P], F32, name="ident")
+        make_identity(nc, ident[:])
+
+        def quantise_weight(w_raw, name):
+            w_grp = const.tile([P, INNER * PASSES * PACK], BF16, name=name + "_grp", align_bytes=64)
+            w_codes = const.tile([P, INNER * PASSES], U32, name=name + "_codes", align_bytes=64)
+            w_scales = const.tile([P, INNER * PASSES], U8, name=name + "_scales", align_bytes=64)
+            src = w_raw[:].rearrange("q (g t h c) -> q h g c t", g=PASSES, t=PACK, h=HEADS)
+            dst = w_grp[:].rearrange("q (h g c t) -> q h g c t", h=HEADS, g=PASSES, t=PACK)
+            for h in range(HEADS):
+                nc.vector.tensor_copy(out=dst[:, h], in_=src[:, h])
+            width = PASSES * DH
+            for h in range(HEADS):
+                nc.vector.quantize_mx(
+                    out=w_codes[:, h * width : (h + 1) * width].bitcast(FP8X4),
+                    scales=w_scales[:, h * width : (h + 1) * width],
+                    in_=w_grp[:, h * width * PACK : (h + 1) * width * PACK],
+                )
+            return w_codes, w_scales
+
+        def transpose_window(w):
+            words = x_tiles[w][:].bitcast(F32)
+            x_grp = stage.tile([P, TOKENS * PASSES * PACK], BF16, name="x_grp", align_bytes=64)
+            x_grp_words = x_grp[:].bitcast(F32).rearrange(
+                "q (j g m u) -> q j g m u", j=PACK, g=PASSES, u=PAIRS
+            )
+            for j in range(PACK):
+                xt = psum.tile([P, PASSES * PAIRS, P], F32, name="xt", tag="bank")
+                for b in range(PASSES * PAIRS):
+                    first = (j * PASSES * PAIRS + b) * P
+                    nc.tensor.transpose(
+                        out=xt[:, b, :], in_=words[:, first : first + P], identity=ident[:]
+                    )
+                nc.scalar.copy(
+                    out=x_grp_words[:, j], in_=xt[:].rearrange("q (g u) m -> q g m u", u=PAIRS)
+                )
+            x_codes = stage.tile([P, TOKENS * PASSES], U32, name="x_codes", align_bytes=64)
+            x_scales = stage.tile([P, TOKENS * PASSES], U8, name="x_scales", align_bytes=64)
+            nc.vector.quantize_mx(out=x_codes[:].bitcast(FP8X4), scales=x_scales[:], in_=x_grp[:])
+            return x_codes, x_scales
+
+        def project(x_q, w_q, h):
+            x_codes, x_scales = x_q
+            w_codes, w_scales = w_q
+            acc = psum.tile([P, PACK, DH], F32, name="acc", tag="bank")
+            for j in range(PACK):
+                for g in range(PASSES):
+                    tok = slice((j * PASSES + g) * P, (j * PASSES + g + 1) * P)
+                    col = slice((h * PASSES + g) * DH, (h * PASSES + g + 1) * DH)
+                    nc.tensor.matmul_mx(
+                        out=acc[:, j, :],
+                        lhsT=x_codes[:, tok].bitcast(FP8X4),
+                        lhsT_scale=x_scales[:, tok],
+                        rhs=w_codes[:, col].bitcast(FP8X4),
+                        rhs_scale=w_scales[:, col],
+                        start=(g == 0),
+                        stop=(g == PASSES - 1),
+                    )
+            return acc
+
+        def project_window(x_q, wk_q, wv_q):
+            kf_grp = stage.tile([P, INNER * PACK], BF16, name="kf_grp", align_bytes=64)
+            v_grp = stage.tile([P, INNER * PACK], BF16, name="v_grp", align_bytes=64)
+            kf_view = kf_grp[:].rearrange("p (h d j) -> p h d j", h=HEADS, j=PACK)
+            v_view = v_grp[:].rearrange("p (h d j) -> p h d j", h=HEADS, j=PACK)
+            for h in range(HEADS):
+                k_acc = project(x_q, wk_q, h)
+                k_by_column = k_acc[:].rearrange("p j d -> p d j")
+                e = exps.tile([P, DH, PACK], F32, name="e")
+                nc.scalar.activation(out=e[:], in_=k_by_column, func=ACT.Exp)
+                nc.vector.tensor_scalar_min(out=e[:], in0=e[:], scalar1=1.0)
+                nc.vector.scalar_tensor_tensor(
+                    out=kf_view[:, h], in0=k_by_column, scalar=0.0, in1=e[:],
+                    op0=ALU.max, op1=ALU.add,
+                )
+            kf_codes = stage.tile([P, INNER], U32, name="kf_codes", align_bytes=64)
+            kf_scales = stage.tile([P, INNER], U8, name="kf_scales", align_bytes=64)
+            nc.vector.quantize_mx(out=kf_codes[:].bitcast(FP8X4), scales=kf_scales[:], in_=kf_grp[:])
+            for h in range(HEADS):
+                v_acc = project(x_q, wv_q, h)
+                nc.scalar.copy(out=v_view[:, h], in_=v_acc[:].rearrange("p j d -> p d j"))
+            v_codes = stage.tile([P, INNER], U32, name="v_codes", align_bytes=64)
+            v_scales = stage.tile([P, INNER], U8, name="v_scales", align_bytes=64)
+            nc.vector.quantize_mx(out=v_codes[:].bitcast(FP8X4), scales=v_scales[:], in_=v_grp[:])
+            return kf_codes, kf_scales, v_codes, v_scales
+
+        def context_window(w, kv_q):
+            kf_codes, kf_scales, v_codes, v_scales = kv_q
+            c_acc = psum.tile([P, HEADS, DH], F32, name="c_acc", tag="bank")
+            for h in range(HEADS):
+                col = slice(h * DH, (h + 1) * DH)
+                nc.tensor.matmul_mx(
+                    out=c_acc[:, h, :],
+                    lhsT=kf_codes[:, col].bitcast(FP8X4),
+                    lhsT_scale=kf_scales[:, col],
+                    rhs=v_codes[:, col].bitcast(FP8X4),
+                    rhs_scale=v_scales[:, col],
+                    start=True,
+                    stop=True,
+                )
+            c_sb = stage.tile([P, HEADS, DH], F32, name="c_sb")
+            nc.vector.tensor_copy(out=c_sb[:], in_=c_acc[:])
+            nc.sync.dma_start(out=out[w].rearrange("h d e -> d h e"), in_=c_sb[:])
+
+        wk_q = quantise_weight(wk_raw, "wk")
+        x_q = transpose_window(0)
+        wv_q = quantise_weight(wv_raw, "wv")
+        kv_q = None
+        for w in range(WINDOWS):
+            x_next = transpose_window(w + 1) if w + 1 < WINDOWS else None
+            kv_next = project_window(x_q, wk_q, wv_q)
+            if w > 0:
+                context_window(w - 1, kv_q)
+            x_q, kv_q = x_next, kv_next
+        context_window(WINDOWS - 1, kv_q)

@@ -22,6 +22,7 @@ HEADS = 4
 DH = 128
 INNER = HEADS * DH
 PAIRS = 2
+RUN = 4
 
 FLOPS = 2 * WINDOWS * TOKENS * FEATURES * 2 * INNER + 2 * WINDOWS * HEADS * TOKENS * DH * DH
 
@@ -29,6 +30,7 @@ FLOPS = 2 * WINDOWS * TOKENS * FEATURES * 2 * INNER + 2 * WINDOWS * HEADS * TOKE
 def tile_localcontextprocessor_pa_t_kernel(tc, x, w_k, w_v, out):
     nc = tc.nc
     with ExitStack() as ctx:
+        ctx.enter_context(tc.manual_schedule())
         const = ctx.enter_context(tc.tile_pool(name="const", bufs=1))
         rows = ctx.enter_context(tc.tile_pool(name="rows", bufs=WINDOWS))
         stage = ctx.enter_context(tc.tile_pool(name="stage", bufs=2))
@@ -63,10 +65,18 @@ def tile_localcontextprocessor_pa_t_kernel(tc, x, w_k, w_v, out):
             w_grp = const.tile([P, INNER * PASSES * PACK], BF16, name=name + "_grp", align_bytes=64)
             w_codes = const.tile([P, INNER * PASSES], U32, name=name + "_codes", align_bytes=64)
             w_scales = const.tile([P, INNER * PASSES], U8, name=name + "_scales", align_bytes=64)
-            src = w_raw[:].rearrange("q (g t h c) -> q h g c t", g=PASSES, t=PACK, h=HEADS)
-            dst = w_grp[:].rearrange("q (h g c t) -> q h g c t", h=HEADS, g=PASSES, t=PACK)
+            src = w_raw[:].rearrange(
+                "q (g t h c i) -> q h g c t i", g=PASSES, t=PACK, h=HEADS, i=RUN
+            )
+            dst = w_grp[:].rearrange(
+                "q (h g c i t) -> q h g c t i", h=HEADS, g=PASSES, i=RUN, t=PACK
+            )
             for h in range(HEADS):
-                nc.vector.tensor_copy(out=dst[:, h], in_=src[:, h])
+                for g in range(PASSES):
+                    if h % 2 == 0:
+                        nc.vector.tensor_copy(out=dst[:, h, g], in_=src[:, h, g])
+                    else:
+                        nc.scalar.copy(out=dst[:, h, g], in_=src[:, h, g])
             width = PASSES * DH
             for h in range(HEADS):
                 nc.vector.quantize_mx(
@@ -79,6 +89,8 @@ def tile_localcontextprocessor_pa_t_kernel(tc, x, w_k, w_v, out):
         def transpose_window(w):
             words = x_tiles[w][:].bitcast(F32)
             x_grp = stage.tile([P, TOKENS * PASSES * PACK], BF16, name="x_grp", align_bytes=64)
+            x_codes = stage.tile([P, TOKENS * PASSES], U32, name="x_codes", align_bytes=64)
+            x_scales = stage.tile([P, TOKENS * PASSES], U8, name="x_scales", align_bytes=64)
             x_grp_words = x_grp[:].bitcast(F32).rearrange(
                 "q (j g m u) -> q j g m u", j=PACK, g=PASSES, u=PAIRS
             )
@@ -92,9 +104,13 @@ def tile_localcontextprocessor_pa_t_kernel(tc, x, w_k, w_v, out):
                 nc.scalar.copy(
                     out=x_grp_words[:, j], in_=xt[:].rearrange("q (g u) m -> q g m u", u=PAIRS)
                 )
-            x_codes = stage.tile([P, TOKENS * PASSES], U32, name="x_codes", align_bytes=64)
-            x_scales = stage.tile([P, TOKENS * PASSES], U8, name="x_scales", align_bytes=64)
-            nc.vector.quantize_mx(out=x_codes[:].bitcast(FP8X4), scales=x_scales[:], in_=x_grp[:])
+            width = PASSES * P
+            for j in range(PACK):
+                nc.vector.quantize_mx(
+                    out=x_codes[:, j * width : (j + 1) * width].bitcast(FP8X4),
+                    scales=x_scales[:, j * width : (j + 1) * width],
+                    in_=x_grp[:, j * width * PACK : (j + 1) * width * PACK],
+                )
             return x_codes, x_scales
 
         def project(x_q, w_q, h):
@@ -116,43 +132,56 @@ def tile_localcontextprocessor_pa_t_kernel(tc, x, w_k, w_v, out):
                     )
             return acc
 
-        def project_window(x_q, wk_q, wv_q):
-            kf_grp = stage.tile([P, INNER * PACK], BF16, name="kf_grp", align_bytes=64)
-            v_grp = stage.tile([P, INNER * PACK], BF16, name="v_grp", align_bytes=64)
-            kf_view = kf_grp[:].rearrange("p (h d j) -> p h d j", h=HEADS, j=PACK)
-            v_view = v_grp[:].rearrange("p (h d j) -> p h d j", h=HEADS, j=PACK)
+        def token_operand(name):
+            grp = stage.tile([P, INNER * PACK], BF16, name=name + "_grp", align_bytes=64)
+            codes = stage.tile([P, INNER], U32, name=name + "_codes", align_bytes=64)
+            scales = stage.tile([P, INNER], U8, name=name + "_scales", align_bytes=64)
+            return grp, codes, scales
+
+        def head_view(operand, h):
+            return operand[0][:].rearrange("p (h d j) -> p h d j", h=HEADS, j=PACK)[:, h]
+
+        def quantise_head(operand, h):
+            grp, codes, scales = operand
+            nc.vector.quantize_mx(
+                out=codes[:, h * DH : (h + 1) * DH].bitcast(FP8X4),
+                scales=scales[:, h * DH : (h + 1) * DH],
+                in_=grp[:, h * DH * PACK : (h + 1) * DH * PACK],
+            )
+
+        def keys(x_q, wk_q):
+            kf = token_operand("kf")
             for h in range(HEADS):
-                k_acc = project(x_q, wk_q, h)
-                k_by_column = k_acc[:].rearrange("p j d -> p d j")
-                e = exps.tile([P, DH, PACK], F32, name="e")
+                k_by_column = project(x_q, wk_q, h)[:].rearrange("p j d -> p d j")
+                e = exps.tile([P, DH, PACK], BF16, name="e")
                 nc.scalar.activation(out=e[:], in_=k_by_column, func=ACT.Exp)
                 nc.vector.tensor_scalar_min(out=e[:], in0=e[:], scalar1=1.0)
+                if h > 0:
+                    quantise_head(kf, h - 1)
                 nc.vector.scalar_tensor_tensor(
-                    out=kf_view[:, h], in0=k_by_column, scalar=0.0, in1=e[:],
+                    out=head_view(kf, h), in0=k_by_column, scalar=0.0, in1=e[:],
                     op0=ALU.max, op1=ALU.add,
                 )
-            kf_codes = stage.tile([P, INNER], U32, name="kf_codes", align_bytes=64)
-            kf_scales = stage.tile([P, INNER], U8, name="kf_scales", align_bytes=64)
-            nc.vector.quantize_mx(out=kf_codes[:].bitcast(FP8X4), scales=kf_scales[:], in_=kf_grp[:])
+            return kf
+
+        def values(x_q, wv_q):
+            v = token_operand("v")
             for h in range(HEADS):
                 v_acc = project(x_q, wv_q, h)
-                nc.scalar.copy(out=v_view[:, h], in_=v_acc[:].rearrange("p j d -> p d j"))
-            v_codes = stage.tile([P, INNER], U32, name="v_codes", align_bytes=64)
-            v_scales = stage.tile([P, INNER], U8, name="v_scales", align_bytes=64)
-            nc.vector.quantize_mx(out=v_codes[:].bitcast(FP8X4), scales=v_scales[:], in_=v_grp[:])
-            return kf_codes, kf_scales, v_codes, v_scales
+                nc.scalar.copy(out=head_view(v, h), in_=v_acc[:].rearrange("p j d -> p d j"))
+                quantise_head(v, h)
+            return v
 
-        def context_window(w, kv_q):
-            kf_codes, kf_scales, v_codes, v_scales = kv_q
+        def context_window(w, kf, v):
             c_acc = psum.tile([P, HEADS, DH], F32, name="c_acc", tag="bank")
             for h in range(HEADS):
                 col = slice(h * DH, (h + 1) * DH)
                 nc.tensor.matmul_mx(
                     out=c_acc[:, h, :],
-                    lhsT=kf_codes[:, col].bitcast(FP8X4),
-                    lhsT_scale=kf_scales[:, col],
-                    rhs=v_codes[:, col].bitcast(FP8X4),
-                    rhs_scale=v_scales[:, col],
+                    lhsT=kf[1][:, col].bitcast(FP8X4),
+                    lhsT_scale=kf[2][:, col],
+                    rhs=v[1][:, col].bitcast(FP8X4),
+                    rhs_scale=v[2][:, col],
                     start=True,
                     stop=True,
                 )
@@ -163,11 +192,13 @@ def tile_localcontextprocessor_pa_t_kernel(tc, x, w_k, w_v, out):
         wk_q = quantise_weight(wk_raw, "wk")
         x_q = transpose_window(0)
         wv_q = quantise_weight(wv_raw, "wv")
-        kv_q = None
+        kf_before, v_before = None, None
         for w in range(WINDOWS):
+            kf = keys(x_q, wk_q)
             x_next = transpose_window(w + 1) if w + 1 < WINDOWS else None
-            kv_next = project_window(x_q, wk_q, wv_q)
+            quantise_head(kf, HEADS - 1)
             if w > 0:
-                context_window(w - 1, kv_q)
-            x_q, kv_q = x_next, kv_next
-        context_window(WINDOWS - 1, kv_q)
+                context_window(w - 1, kf_before, v_before)
+            v = values(x_q, wv_q)
+            x_q, kf_before, v_before = x_next, kf, v
+        context_window(WINDOWS - 1, kf_before, v_before)

@@ -37,19 +37,27 @@ def tile_localcontextprocessor_pa_t_kernel(tc, x, w_k, w_v, out):
         exps = ctx.enter_context(tc.tile_pool(name="exps", bufs=4))
         psum = ctx.enter_context(tc.psum_pool(name="psum", bufs=8))
 
-        x_windows = x.rearrange("b (n p j) d -> (b n) p (j d)", n=2, p=P, j=PACK)
+        x_windows = x.rearrange("b (n p j) d -> (b n) j p d", n=2, p=P, j=PACK)
 
         def load_window(w):
             x_rows = rows.tile([P, PACK * FEATURES], BF16, name="x_rows")
-            nc.sync.dma_start(out=x_rows[:], in_=x_windows[w])
+            for j in range(PACK):
+                nc.sync.dma_start(
+                    out=x_rows[:, j * FEATURES : (j + 1) * FEATURES], in_=x_windows[w, j]
+                )
             return x_rows
 
         def load_weight(w_dram, name):
             w_raw = const.tile([P, PASSES * PACK * INNER], BF16, name=name)
-            nc.sync.dma_start(
-                out=w_raw[:].rearrange("q (s r) -> q s r", s=PASSES * PAIRS),
-                in_=w_dram.rearrange("(s q e) c -> q s (e c)", s=PASSES * PAIRS, q=P, e=2),
-            )
+            for g in range(PASSES):
+                nc.sync.dma_start(
+                    out=w_raw[:, g * PACK * INNER : (g + 1) * PACK * INNER].rearrange(
+                        "q (u r) -> q u r", u=PAIRS
+                    ),
+                    in_=w_dram[g * K_PASS : (g + 1) * K_PASS, :].rearrange(
+                        "(u q e) c -> q u (e c)", u=PAIRS, q=P, e=2
+                    ),
+                )
             return w_raw
 
         wk_raw = load_weight(w_k, "wk_raw")
@@ -61,7 +69,11 @@ def tile_localcontextprocessor_pa_t_kernel(tc, x, w_k, w_v, out):
         ident = const.tile([P, P], F32, name="ident")
         make_identity(nc, ident[:])
 
-        def quantise_weight(w_raw, name):
+        warm = const.tile([P, 1], F32, name="warm")
+        nc.vector.memset(warm[:], 0.0)
+        nc.scalar.activation(out=warm[:], in_=warm[:], func=ACT.Exp)
+
+        def quantise_weight(w_raw, name, scalar_helps):
             w_grp = const.tile([P, INNER * PASSES * PACK], BF16, name=name + "_grp", align_bytes=64)
             w_codes = const.tile([P, INNER * PASSES], U32, name=name + "_codes", align_bytes=64)
             w_scales = const.tile([P, INNER * PASSES], U8, name=name + "_scales", align_bytes=64)
@@ -71,12 +83,12 @@ def tile_localcontextprocessor_pa_t_kernel(tc, x, w_k, w_v, out):
             dst = w_grp[:].rearrange(
                 "q (h g c i t) -> q h g c t i", h=HEADS, g=PASSES, i=RUN, t=PACK
             )
-            for h in range(HEADS):
-                for g in range(PASSES):
-                    if h % 2 == 0:
-                        nc.vector.tensor_copy(out=dst[:, h, g], in_=src[:, h, g])
-                    else:
+            for g in range(PASSES):
+                for h in range(HEADS):
+                    if scalar_helps and h % 2 == 1:
                         nc.scalar.copy(out=dst[:, h, g], in_=src[:, h, g])
+                    else:
+                        nc.vector.tensor_copy(out=dst[:, h, g], in_=src[:, h, g])
             width = PASSES * DH
             for h in range(HEADS):
                 nc.vector.quantize_mx(
@@ -189,9 +201,9 @@ def tile_localcontextprocessor_pa_t_kernel(tc, x, w_k, w_v, out):
             nc.vector.tensor_copy(out=c_sb[:], in_=c_acc[:])
             nc.sync.dma_start(out=out[w].rearrange("h d e -> d h e"), in_=c_sb[:])
 
-        wk_q = quantise_weight(wk_raw, "wk")
+        wk_q = quantise_weight(wk_raw, "wk", True)
         x_q = transpose_window(0)
-        wv_q = quantise_weight(wv_raw, "wv")
+        wv_q = quantise_weight(wv_raw, "wv", True)
         kf_before, v_before = None, None
         for w in range(WINDOWS):
             kf = keys(x_q, wk_q)

@@ -22,6 +22,7 @@ HEADS = 4
 DH = 128
 INNER = HEADS * DH
 PAIRS = 2
+HALF = 2
 RUN = 4
 
 FLOPS = 2 * WINDOWS * TOKENS * FEATURES * 2 * INNER + 2 * WINDOWS * HEADS * TOKENS * DH * DH
@@ -38,33 +39,37 @@ def tile_localcontextprocessor_pa_t_kernel(tc, x, w_k, w_v, out):
         psum = ctx.enter_context(tc.psum_pool(name="psum", bufs=8))
 
         x_windows = x.rearrange("b (n p j) d -> (b n) j p d", n=2, p=P, j=PACK)
+        x_tiles = [
+            rows.tile([P, PACK * FEATURES], BF16, name="x_rows") for w in range(WINDOWS)
+        ]
 
-        def load_window(w):
-            x_rows = rows.tile([P, PACK * FEATURES], BF16, name="x_rows")
-            for j in range(PACK):
-                nc.sync.dma_start(
-                    out=x_rows[:, j * FEATURES : (j + 1) * FEATURES], in_=x_windows[w, j]
-                )
-            return x_rows
+        def load_token_tile(w, j):
+            nc.sync.dma_start(
+                out=x_tiles[w][:, j * FEATURES : (j + 1) * FEATURES], in_=x_windows[w, j]
+            )
 
-        def load_weight(w_dram, name):
-            w_raw = const.tile([P, PASSES * PACK * INNER], BF16, name=name)
-            for g in range(PASSES):
-                nc.sync.dma_start(
-                    out=w_raw[:, g * PACK * INNER : (g + 1) * PACK * INNER].rearrange(
-                        "q (u r) -> q u r", u=PAIRS
-                    ),
-                    in_=w_dram[g * K_PASS : (g + 1) * K_PASS, :].rearrange(
-                        "(u q e) c -> q u (e c)", u=PAIRS, q=P, e=2
-                    ),
-                )
-            return w_raw
+        wk_raw = const.tile([P, PASSES * PACK * INNER], BF16, name="wk_raw")
+        wv_raw = const.tile([P, PASSES * PACK * INNER], BF16, name="wv_raw")
 
-        wk_raw = load_weight(w_k, "wk_raw")
-        x_tiles = [load_window(0)]
-        wv_raw = load_weight(w_v, "wv_raw")
+        def load_weight_pass(w_raw, w_dram, g):
+            nc.sync.dma_start(
+                out=w_raw[:, g * PACK * INNER : (g + 1) * PACK * INNER].rearrange(
+                    "q (u r) -> q u r", u=PAIRS
+                ),
+                in_=w_dram[g * K_PASS : (g + 1) * K_PASS, :].rearrange(
+                    "(u q e) c -> q u (e c)", u=PAIRS, q=P, e=2
+                ),
+            )
+
+        for g in range(PASSES):
+            load_weight_pass(wk_raw, w_k, g)
+        for j in range(PACK):
+            load_token_tile(0, j)
+        for g in range(PASSES):
+            load_weight_pass(wv_raw, w_v, g)
         for w in range(1, WINDOWS):
-            x_tiles.append(load_window(w))
+            for j in range(PACK):
+                load_token_tile(w, j)
 
         ident = const.tile([P, P], F32, name="ident")
         make_identity(nc, ident[:])
@@ -73,75 +78,80 @@ def tile_localcontextprocessor_pa_t_kernel(tc, x, w_k, w_v, out):
         nc.vector.memset(warm[:], 0.0)
         nc.scalar.activation(out=warm[:], in_=warm[:], func=ACT.Exp)
 
-        def quantise_weight(w_raw, name, scalar_helps):
-            w_grp = const.tile([P, INNER * PASSES * PACK], BF16, name=name + "_grp", align_bytes=64)
-            w_codes = const.tile([P, INNER * PASSES], U32, name=name + "_codes", align_bytes=64)
-            w_scales = const.tile([P, INNER * PASSES], U8, name=name + "_scales", align_bytes=64)
-            src = w_raw[:].rearrange(
-                "q (g t h c i) -> q h g c t i", g=PASSES, t=PACK, h=HEADS, i=RUN
-            )
-            dst = w_grp[:].rearrange(
-                "q (h g c i t) -> q h g c t i", h=HEADS, g=PASSES, i=RUN, t=PACK
-            )
-            for g in range(PASSES):
-                for h in range(HEADS):
-                    if scalar_helps and h % 2 == 1:
-                        nc.scalar.copy(out=dst[:, h, g], in_=src[:, h, g])
-                    else:
-                        nc.vector.tensor_copy(out=dst[:, h, g], in_=src[:, h, g])
-            width = PASSES * DH
-            for h in range(HEADS):
-                nc.vector.quantize_mx(
-                    out=w_codes[:, h * width : (h + 1) * width].bitcast(FP8X4),
-                    scales=w_scales[:, h * width : (h + 1) * width],
-                    in_=w_grp[:, h * width * PACK : (h + 1) * width * PACK],
-                )
-            return w_codes, w_scales
+        def weight_operand(name):
+            grp = const.tile([P, PASSES * INNER * PACK], BF16, name=name + "_grp", align_bytes=64)
+            codes = const.tile([P, PASSES * INNER], U32, name=name + "_codes", align_bytes=64)
+            scales = const.tile([P, PASSES * INNER], U8, name=name + "_scales", align_bytes=64)
+            return grp, codes, scales
 
-        def transpose_window(w):
-            words = x_tiles[w][:].bitcast(F32)
+        def regroup_weight(w_q, w_raw, g, scalar_heads):
+            src = w_raw[:].rearrange(
+                "q (g t h c i) -> q g h c t i", g=PASSES, t=PACK, h=HEADS, i=RUN
+            )
+            dst = w_q[0][:].rearrange(
+                "q (g h c i t) -> q g h c t i", h=HEADS, g=PASSES, i=RUN, t=PACK
+            )
+            for h in range(HEADS):
+                if h in scalar_heads:
+                    nc.scalar.copy(out=dst[:, g, h], in_=src[:, g, h])
+                else:
+                    nc.vector.tensor_copy(out=dst[:, g, h], in_=src[:, g, h])
+
+        def quantise(operand, first, count):
+            grp, codes, scales = operand
+            nc.vector.quantize_mx(
+                out=codes[:, first : first + count].bitcast(FP8X4),
+                scales=scales[:, first : first + count],
+                in_=grp[:, first * PACK : (first + count) * PACK],
+            )
+
+        def window_operand():
             x_grp = stage.tile([P, TOKENS * PASSES * PACK], BF16, name="x_grp", align_bytes=64)
             x_codes = stage.tile([P, TOKENS * PASSES], U32, name="x_codes", align_bytes=64)
             x_scales = stage.tile([P, TOKENS * PASSES], U8, name="x_scales", align_bytes=64)
-            x_grp_words = x_grp[:].bitcast(F32).rearrange(
+            return x_grp, x_codes, x_scales
+
+        def transpose_tile(x_q, w, j, on_vector):
+            words = x_tiles[w][:].bitcast(F32)
+            x_grp_words = x_q[0][:].bitcast(F32).rearrange(
                 "q (j g m u) -> q j g m u", j=PACK, g=PASSES, u=PAIRS
             )
-            for j in range(PACK):
-                xt = psum.tile([P, PASSES * PAIRS, P], F32, name="xt", tag="bank")
-                for b in range(PASSES * PAIRS):
-                    first = (j * PASSES * PAIRS + b) * P
-                    nc.tensor.transpose(
-                        out=xt[:, b, :], in_=words[:, first : first + P], identity=ident[:]
-                    )
-                nc.scalar.copy(
-                    out=x_grp_words[:, j], in_=xt[:].rearrange("q (g u) m -> q g m u", u=PAIRS)
+            xt = psum.tile([P, PASSES * PAIRS, P], F32, name="xt", tag="bank")
+            for b in range(PASSES * PAIRS):
+                first = (j * PASSES * PAIRS + b) * P
+                nc.tensor.transpose(
+                    out=xt[:, b, :], in_=words[:, first : first + P], identity=ident[:]
                 )
-            width = PASSES * P
-            for j in range(PACK):
-                nc.vector.quantize_mx(
-                    out=x_codes[:, j * width : (j + 1) * width].bitcast(FP8X4),
-                    scales=x_scales[:, j * width : (j + 1) * width],
-                    in_=x_grp[:, j * width * PACK : (j + 1) * width * PACK],
+            x_words = xt[:].rearrange("q (g u) m -> q g m u", u=PAIRS)
+            if on_vector:
+                nc.vector.tensor_copy(out=x_grp_words[:, j], in_=x_words)
+            else:
+                nc.scalar.copy(out=x_grp_words[:, j], in_=x_words)
+
+        def quantise_tiles(x_q, j, count):
+            quantise(x_q, j * PASSES * P, count * PASSES * P)
+
+        def project_tile(acc, x_q, w_q, h, j):
+            for g in range(PASSES):
+                tok = slice((j * PASSES + g) * P, (j * PASSES + g + 1) * P)
+                col = slice((g * HEADS + h) * DH, (g * HEADS + h + 1) * DH)
+                nc.tensor.matmul_mx(
+                    out=acc[:, j, :],
+                    lhsT=x_q[1][:, tok].bitcast(FP8X4),
+                    lhsT_scale=x_q[2][:, tok],
+                    rhs=w_q[1][:, col].bitcast(FP8X4),
+                    rhs_scale=w_q[2][:, col],
+                    start=(g == 0),
+                    stop=(g == PASSES - 1),
                 )
-            return x_codes, x_scales
+
+        def new_bank():
+            return psum.tile([P, PACK, DH], F32, name="acc", tag="bank")
 
         def project(x_q, w_q, h):
-            x_codes, x_scales = x_q
-            w_codes, w_scales = w_q
-            acc = psum.tile([P, PACK, DH], F32, name="acc", tag="bank")
+            acc = new_bank()
             for j in range(PACK):
-                for g in range(PASSES):
-                    tok = slice((j * PASSES + g) * P, (j * PASSES + g + 1) * P)
-                    col = slice((h * PASSES + g) * DH, (h * PASSES + g + 1) * DH)
-                    nc.tensor.matmul_mx(
-                        out=acc[:, j, :],
-                        lhsT=x_codes[:, tok].bitcast(FP8X4),
-                        lhsT_scale=x_scales[:, tok],
-                        rhs=w_codes[:, col].bitcast(FP8X4),
-                        rhs_scale=w_scales[:, col],
-                        start=(g == 0),
-                        stop=(g == PASSES - 1),
-                    )
+                project_tile(acc, x_q, w_q, h, j)
             return acc
 
         def token_operand(name):
@@ -150,46 +160,33 @@ def tile_localcontextprocessor_pa_t_kernel(tc, x, w_k, w_v, out):
             scales = stage.tile([P, INNER], U8, name=name + "_scales", align_bytes=64)
             return grp, codes, scales
 
+        def by_column(acc):
+            return acc[:].rearrange("p j d -> p d j")
+
         def head_view(operand, h):
             return operand[0][:].rearrange("p (h d j) -> p h d j", h=HEADS, j=PACK)[:, h]
 
-        def quantise_head(operand, h):
-            grp, codes, scales = operand
-            nc.vector.quantize_mx(
-                out=codes[:, h * DH : (h + 1) * DH].bitcast(FP8X4),
-                scales=scales[:, h * DH : (h + 1) * DH],
-                in_=grp[:, h * DH * PACK : (h + 1) * DH * PACK],
+        def quantise_heads(operand, h, count):
+            quantise(operand, h * DH, count * DH)
+
+        def exp_head(e, i, acc):
+            nc.scalar.activation(out=e[:, i], in_=by_column(acc), func=ACT.Exp)
+
+        def add_head(kf, h, acc, e, i):
+            nc.vector.scalar_tensor_tensor(
+                out=head_view(kf, h), in0=by_column(acc), scalar=0.0, in1=e[:, i],
+                op0=ALU.max, op1=ALU.add,
             )
 
-        def keys(x_q, wk_q):
-            kf = token_operand("kf")
-            for h in range(HEADS):
-                k_by_column = project(x_q, wk_q, h)[:].rearrange("p j d -> p d j")
-                e = exps.tile([P, DH, PACK], BF16, name="e")
-                nc.scalar.activation(out=e[:], in_=k_by_column, func=ACT.Exp)
-                nc.vector.tensor_scalar_min(out=e[:], in0=e[:], scalar1=1.0)
-                if h > 0:
-                    quantise_head(kf, h - 1)
-                nc.vector.scalar_tensor_tensor(
-                    out=head_view(kf, h), in0=k_by_column, scalar=0.0, in1=e[:],
-                    op0=ALU.max, op1=ALU.add,
-                )
-            return kf
+        def clip(e):
+            nc.vector.tensor_scalar_min(out=e[:], in0=e[:], scalar1=1.0)
 
-        def values(x_q, wv_q):
-            v = token_operand("v")
-            for h in range(HEADS):
-                v_acc = project(x_q, wv_q, h)
-                nc.scalar.copy(out=head_view(v, h), in_=v_acc[:].rearrange("p j d -> p d j"))
-                quantise_head(v, h)
-            return v
-
-        def context_window(w, kf, v):
-            c_acc = psum.tile([P, HEADS, DH], F32, name="c_acc", tag="bank")
-            for h in range(HEADS):
-                col = slice(h * DH, (h + 1) * DH)
+        def context_heads(w, kf, v, first, count):
+            c_acc = psum.tile([P, count, DH], F32, name="c_acc", tag="bank")
+            for i in range(count):
+                col = slice((first + i) * DH, (first + i + 1) * DH)
                 nc.tensor.matmul_mx(
-                    out=c_acc[:, h, :],
+                    out=c_acc[:, i, :],
                     lhsT=kf[1][:, col].bitcast(FP8X4),
                     lhsT_scale=kf[2][:, col],
                     rhs=v[1][:, col].bitcast(FP8X4),
@@ -197,20 +194,80 @@ def tile_localcontextprocessor_pa_t_kernel(tc, x, w_k, w_v, out):
                     start=True,
                     stop=True,
                 )
-            c_sb = stage.tile([P, HEADS, DH], F32, name="c_sb")
-            nc.vector.tensor_copy(out=c_sb[:], in_=c_acc[:])
-            nc.sync.dma_start(out=out[w].rearrange("h d e -> d h e"), in_=c_sb[:])
+            return c_acc
 
-        wk_q = quantise_weight(wk_raw, "wk", True)
-        x_q = transpose_window(0)
-        wv_q = quantise_weight(wv_raw, "wv", True)
+        def store_context(w, c_acc, first, count, on_scalar=False):
+            c_sb = stage.tile([P, count, DH], F32, name="c_sb")
+            if on_scalar:
+                nc.scalar.copy(out=c_sb[:], in_=c_acc[:])
+            else:
+                nc.vector.tensor_copy(out=c_sb[:], in_=c_acc[:])
+            nc.sync.dma_start(
+                out=out[w, first : first + count].rearrange("h d e -> d h e"), in_=c_sb[:]
+            )
+
+        wk_q = weight_operand("wk")
+        wv_q = weight_operand("wv")
+        x_q = window_operand()
+        for g in range(PASSES):
+            regroup_weight(wk_q, wk_raw, g, (1, 3))
+        for j in range(PACK):
+            transpose_tile(x_q, 0, j, False)
+        for g in range(PASSES):
+            for h in range(0, HEADS, HALF):
+                quantise(wk_q, (g * HEADS + h) * DH, HALF * DH)
+        for j in range(PACK):
+            quantise_tiles(x_q, j, 1)
+        for g in range(PASSES):
+            regroup_weight(wv_q, wv_raw, g, (1, 3))
+        for g in range(PASSES):
+            quantise(wv_q, g * INNER, INNER)
         kf_before, v_before = None, None
         for w in range(WINDOWS):
-            kf = keys(x_q, wk_q)
-            x_next = transpose_window(w + 1) if w + 1 < WINDOWS else None
-            quantise_head(kf, HEADS - 1)
+            last = w + 1 == WINDOWS
+
+            kf = token_operand("kf")
+            k_accs, e_tiles = [], []
+            for h in range(HEADS):
+                acc = project(x_q, wk_q, h)
+                e = exps.tile([P, 1, DH, PACK], BF16, name="e")
+                exp_head(e, 0, acc)
+                clip(e)
+                k_accs.append(acc)
+                e_tiles.append(e)
+                if h == 0 and w > 0:
+                    quantise_heads(v_before, HALF, HALF)
+                if h > 0:
+                    add_head(kf, h - 1, k_accs[h - 1], e_tiles[h - 1], 0)
+            quantise_heads(kf, 0, HALF)
+            add_head(kf, HEADS - 1, k_accs[HEADS - 1], e_tiles[HEADS - 1], 0)
+
+            if not last:
+                x_next = window_operand()
+                for j in range(PACK):
+                    transpose_tile(x_next, w + 1, j, False)
+                quantise_tiles(x_next, 0, HALF)
+            quantise_heads(kf, HALF, HALF)
+            if not last:
+                quantise_tiles(x_next, HALF, HALF)
+
             if w > 0:
-                context_window(w - 1, kf_before, v_before)
-            v = values(x_q, wv_q)
+                c_acc = context_heads(w - 1, kf_before, v_before, 0, HEADS)
+                store_context(w - 1, c_acc, 0, HEADS)
+
+            v = token_operand("v")
+            for h in range(HEADS):
+                acc = project(x_q, wv_q, h)
+                if h == HEADS - 1 and not last:
+                    nc.vector.tensor_copy(out=head_view(v, h), in_=by_column(acc))
+                else:
+                    nc.scalar.copy(out=head_view(v, h), in_=by_column(acc))
+                if h == HALF:
+                    quantise_heads(v, 0, HALF)
             x_q, kf_before, v_before = x_next, kf, v
-        context_window(WINDOWS - 1, kf_before, v_before)
+
+        for h in range(HALF, HEADS):
+            quantise_heads(v, h, 1)
+        for first in range(0, HEADS, HALF):
+            c_acc = context_heads(WINDOWS - 1, kf, v, first, HALF)
+            store_context(WINDOWS - 1, c_acc, first, HALF, on_scalar=(first == 0))

@@ -35,6 +35,7 @@ def tile_localcontextprocessor_pa_t_kernel(tc, x, w_k, w_v, out):
         const = ctx.enter_context(tc.tile_pool(name="const", bufs=1))
         rows = ctx.enter_context(tc.tile_pool(name="rows", bufs=WINDOWS))
         stage = ctx.enter_context(tc.tile_pool(name="stage", bufs=2))
+        outs = ctx.enter_context(tc.tile_pool(name="outs", bufs=4))
         exps = ctx.enter_context(tc.tile_pool(name="exps", bufs=4))
         psum = ctx.enter_context(tc.psum_pool(name="psum", bufs=8))
 
@@ -197,7 +198,7 @@ def tile_localcontextprocessor_pa_t_kernel(tc, x, w_k, w_v, out):
             return c_acc
 
         def store_context(w, c_acc, first, count, on_scalar=False):
-            c_sb = stage.tile([P, count, DH], F32, name="c_sb")
+            c_sb = outs.tile([P, count, DH], F32, name="c_sb")
             if on_scalar:
                 nc.scalar.copy(out=c_sb[:], in_=c_acc[:])
             else:
@@ -253,7 +254,7 @@ def tile_localcontextprocessor_pa_t_kernel(tc, x, w_k, w_v, out):
 
             if w > 0:
                 c_acc = context_heads(w - 1, kf_before, v_before, 0, HEADS)
-                store_context(w - 1, c_acc, 0, HEADS)
+                store_context(w - 1, c_acc, 0, HEADS, on_scalar=last)
 
             v = token_operand("v")
             for h in range(HEADS):

@@ -259,10 +259,7 @@ def tile_localcontextprocessor_pa_t_kernel(tc, x, w_k, w_v, out):
             v = token_operand("v")
             for h in range(HEADS):
                 acc = project(x_q, wv_q, h)
-                if h == HEADS - 1 and not last:
-                    nc.vector.tensor_copy(out=head_view(v, h), in_=by_column(acc))
-                else:
-                    nc.scalar.copy(out=head_view(v, h), in_=by_column(acc))
+                nc.scalar.copy(out=head_view(v, h), in_=by_column(acc))
                 if h == HALF:
                     quantise_heads(v, 0, HALF)
             x_q, kf_before, v_before = x_next, kf, v

@@ -34,7 +34,8 @@ def tile_localcontextprocessor_pa_t_kernel(tc, x, w_k, w_v, out):
         ctx.enter_context(tc.manual_schedule())
         const = ctx.enter_context(tc.tile_pool(name="const", bufs=1))
         rows = ctx.enter_context(tc.tile_pool(name="rows", bufs=WINDOWS))
-        stage = ctx.enter_context(tc.tile_pool(name="stage", bufs=2))
+        windows = ctx.enter_context(tc.tile_pool(name="windows", bufs=4))
+        stage = ctx.enter_context(tc.tile_pool(name="stage", bufs=3))
         outs = ctx.enter_context(tc.tile_pool(name="outs", bufs=4))
         exps = ctx.enter_context(tc.tile_pool(name="exps", bufs=4))
         psum = ctx.enter_context(tc.psum_pool(name="psum", bufs=8))
@@ -107,9 +108,9 @@ def tile_localcontextprocessor_pa_t_kernel(tc, x, w_k, w_v, out):
             )
 
         def window_operand():
-            x_grp = stage.tile([P, TOKENS * PASSES * PACK], BF16, name="x_grp", align_bytes=64)
-            x_codes = stage.tile([P, TOKENS * PASSES], U32, name="x_codes", align_bytes=64)
-            x_scales = stage.tile([P, TOKENS * PASSES], U8, name="x_scales", align_bytes=64)
+            x_grp = windows.tile([P, TOKENS * PASSES * PACK], BF16, name="x_grp", align_bytes=64)
+            x_codes = windows.tile([P, TOKENS * PASSES], U32, name="x_codes", align_bytes=64)
+            x_scales = windows.tile([P, TOKENS * PASSES], U8, name="x_scales", align_bytes=64)
             return x_grp, x_codes, x_scales
 
         def transpose_tile(x_q, w, j, on_vector):
@@ -209,63 +210,73 @@ def tile_localcontextprocessor_pa_t_kernel(tc, x, w_k, w_v, out):
 
         wk_q = weight_operand("wk")
         wv_q = weight_operand("wv")
-        x_q = window_operand()
+        x_q = {0: window_operand()}
+        kf, v = {}, {}
         for g in range(PASSES):
             regroup_weight(wk_q, wk_raw, g, (1, 3))
         for j in range(PACK):
-            transpose_tile(x_q, 0, j, False)
+            transpose_tile(x_q[0], 0, j, False)
         for g in range(PASSES):
             for h in range(0, HEADS, HALF):
                 quantise(wk_q, (g * HEADS + h) * DH, HALF * DH)
         for j in range(PACK):
-            quantise_tiles(x_q, j, 1)
+            quantise_tiles(x_q[0], j, 1)
         for g in range(PASSES):
             regroup_weight(wv_q, wv_raw, g, (1, 3))
         for g in range(PASSES):
             quantise(wv_q, g * INNER, INNER)
-        kf_before, v_before = None, None
+
         for w in range(WINDOWS):
             last = w + 1 == WINDOWS
 
-            kf = token_operand("kf")
+            kf[w] = token_operand("kf")
             k_accs, e_tiles = [], []
             for h in range(HEADS):
-                acc = project(x_q, wk_q, h)
+                acc = project(x_q[w], wk_q, h)
                 e = exps.tile([P, 1, DH, PACK], BF16, name="e")
                 exp_head(e, 0, acc)
                 clip(e)
                 k_accs.append(acc)
                 e_tiles.append(e)
-                if h == 0 and w > 0:
-                    quantise_heads(v_before, HALF, HALF)
                 if h > 0:
-                    add_head(kf, h - 1, k_accs[h - 1], e_tiles[h - 1], 0)
-            quantise_heads(kf, 0, HALF)
-            add_head(kf, HEADS - 1, k_accs[HEADS - 1], e_tiles[HEADS - 1], 0)
+                    add_head(kf[w], h - 1, k_accs[h - 1], e_tiles[h - 1], 0)
+            add_head(kf[w], HEADS - 1, k_accs[HEADS - 1], e_tiles[HEADS - 1], 0)
 
-            if not last:
-                x_next = window_operand()
+            if w >= 2:
+                c_acc = context_heads(w - 2, kf[w - 2], v[w - 2], 0, HEADS)
+                store_context(w - 2, c_acc, 0, HEADS, on_scalar=True)
+
+            if w == 0:
+                x_q[1] = window_operand()
                 for j in range(PACK):
-                    transpose_tile(x_next, w + 1, j, False)
-                quantise_tiles(x_next, 0, HALF)
-            quantise_heads(kf, HALF, HALF)
-            if not last:
-                quantise_tiles(x_next, HALF, HALF)
+                    transpose_tile(x_q[1], 1, j, False)
+                for j in range(0, PACK, HALF):
+                    quantise_tiles(x_q[1], j, HALF)
 
             if w > 0:
-                c_acc = context_heads(w - 1, kf_before, v_before, 0, HEADS)
-                store_context(w - 1, c_acc, 0, HEADS, on_scalar=last)
+                quantise_heads(v[w - 1], 0, HEADS)
+            quantise_heads(kf[w], 0, HEADS)
 
-            v = token_operand("v")
+            v[w] = token_operand("v")
             for h in range(HEADS):
-                acc = project(x_q, wv_q, h)
-                nc.scalar.copy(out=head_view(v, h), in_=by_column(acc))
-                if h == HALF:
-                    quantise_heads(v, 0, HALF)
-            x_q, kf_before, v_before = x_next, kf, v
+                acc = project(x_q[w], wv_q, h)
+                nc.scalar.copy(out=head_view(v[w], h), in_=by_column(acc))
 
+            if w % 2 == 0 and w + 2 < WINDOWS:
+                for ahead in (w + 2, w + 3):
+                    x_q[ahead] = window_operand()
+                    for j in range(PACK):
+                        transpose_tile(x_q[ahead], ahead, j, j % 2 == 1)
+                for ahead in (w + 2, w + 3):
+                    for j in range(0, PACK, HALF):
+                        quantise_tiles(x_q[ahead], j, HALF)
+
+        w = WINDOWS - 1
+        c_before = context_heads(w - 1, kf[w - 1], v[w - 1], 0, HEADS)
+        quantise_heads(v[w], 0, HALF)
         for h in range(HALF, HEADS):
-            quantise_heads(v, h, 1)
+            quantise_heads(v[w], h, 1)
+        store_context(w - 1, c_before, 0, HEADS, on_scalar=True)
         for first in range(0, HEADS, HALF):
-            c_acc = context_heads(WINDOWS - 1, kf, v, first, HALF)
-            store_context(WINDOWS - 1, c_acc, first, HALF, on_scalar=(first == 0))
+            c_acc = context_heads(w, kf[w], v[w], first, HALF)
+            store_context(w, c_acc, first, HALF, on_scalar=(first > 0))

@@ -23,6 +23,7 @@ DH = 128
 INNER = HEADS * DH
 PAIRS = 2
 HALF = 2
+RUNS = {0: (2, 3), 2: (4, 5, 6, 7)}
 RUN = 4
 
 FLOPS = 2 * WINDOWS * TOKENS * FEATURES * 2 * INNER + 2 * WINDOWS * HEADS * TOKENS * DH * DH
@@ -34,7 +35,7 @@ def tile_localcontextprocessor_pa_t_kernel(tc, x, w_k, w_v, out):
         ctx.enter_context(tc.manual_schedule())
         const = ctx.enter_context(tc.tile_pool(name="const", bufs=1))
         rows = ctx.enter_context(tc.tile_pool(name="rows", bufs=WINDOWS))
-        windows = ctx.enter_context(tc.tile_pool(name="windows", bufs=4))
+        windows = ctx.enter_context(tc.tile_pool(name="windows", bufs=5))
         stage = ctx.enter_context(tc.tile_pool(name="stage", bufs=3))
         outs = ctx.enter_context(tc.tile_pool(name="outs", bufs=4))
         exps = ctx.enter_context(tc.tile_pool(name="exps", bufs=4))
@@ -133,6 +134,10 @@ def tile_localcontextprocessor_pa_t_kernel(tc, x, w_k, w_v, out):
         def quantise_tiles(x_q, j, count):
             quantise(x_q, j * PASSES * P, count * PASSES * P)
 
+        def quantise_window(x_q):
+            for j in range(0, PACK, HALF):
+                quantise_tiles(x_q, j, HALF)
+
         def project_tile(acc, x_q, w_q, h, j):
             for g in range(PASSES):
                 tok = slice((j * PASSES + g) * P, (j * PASSES + g + 1) * P)
@@ -212,6 +217,7 @@ def tile_localcontextprocessor_pa_t_kernel(tc, x, w_k, w_v, out):
         wv_q = weight_operand("wv")
         x_q = {0: window_operand()}
         kf, v = {}, {}
+        waiting = []
         for g in range(PASSES):
             regroup_weight(wk_q, wk_raw, g, (1, 3))
         for j in range(PACK):
@@ -246,12 +252,14 @@ def tile_localcontextprocessor_pa_t_kernel(tc, x, w_k, w_v, out):
                 c_acc = context_heads(w - 2, kf[w - 2], v[w - 2], 0, HEADS)
                 store_context(w - 2, c_acc, 0, HEADS, on_scalar=True)
 
+            if waiting:
+                quantise_window(x_q[waiting.pop(0)])
+
             if w == 0:
                 x_q[1] = window_operand()
                 for j in range(PACK):
                     transpose_tile(x_q[1], 1, j, False)
-                for j in range(0, PACK, HALF):
-                    quantise_tiles(x_q[1], j, HALF)
+                quantise_window(x_q[1])
 
             if w > 0:
                 quantise_heads(v[w - 1], 0, HEADS)
@@ -262,14 +270,14 @@ def tile_localcontextprocessor_pa_t_kernel(tc, x, w_k, w_v, out):
                 acc = project(x_q[w], wv_q, h)
                 nc.scalar.copy(out=head_view(v[w], h), in_=by_column(acc))
 
-            if w % 2 == 0 and w + 2 < WINDOWS:
-                for ahead in (w + 2, w + 3):
-                    x_q[ahead] = window_operand()
-                    for j in range(PACK):
-                        transpose_tile(x_q[ahead], ahead, j, j % 2 == 1)
-                for ahead in (w + 2, w + 3):
-                    for j in range(0, PACK, HALF):
-                        quantise_tiles(x_q[ahead], j, HALF)
+            run = RUNS.get(w, ())
+            for ahead in run:
+                x_q[ahead] = window_operand()
+                for j in range(PACK):
+                    transpose_tile(x_q[ahead], ahead, j, j % 2 == 1)
+            for ahead in run[:1]:
+                quantise_window(x_q[ahead])
+            waiting += run[1:]
 
         w = WINDOWS - 1
         c_before = context_heads(w - 1, kf[w - 1], v[w - 1], 0, HEADS)

@@ -41,15 +41,14 @@ def tile_localcontextprocessor_pa_t_kernel(tc, x, w_k, w_v, out):
         exps = ctx.enter_context(tc.tile_pool(name="exps", bufs=4))
         psum = ctx.enter_context(tc.psum_pool(name="psum", bufs=8))
 
-        x_windows = x.rearrange("b (n p j) d -> (b n) j p d", n=2, p=P, j=PACK)
+        x_windows = x.rearrange("b (n p j) d -> (b n) p (j d)", n=2, p=P, j=PACK)
         x_tiles = [
             rows.tile([P, PACK * FEATURES], BF16, name="x_rows") for w in range(WINDOWS)
         ]
 
-        def load_token_tile(w, j):
-            nc.sync.dma_start(
-                out=x_tiles[w][:, j * FEATURES : (j + 1) * FEATURES], in_=x_windows[w, j]
-            )
+        def load_tokens(w, j, count):
+            cols = slice(j * FEATURES, (j + count) * FEATURES)
+            nc.sync.dma_start(out=x_tiles[w][:, cols], in_=x_windows[w, :, cols])
 
         wk_raw = const.tile([P, PASSES * PACK * INNER], BF16, name="wk_raw")
         wv_raw = const.tile([P, PASSES * PACK * INNER], BF16, name="wv_raw")
@@ -67,12 +66,13 @@ def tile_localcontextprocessor_pa_t_kernel(tc, x, w_k, w_v, out):
         for g in range(PASSES):
             load_weight_pass(wk_raw, w_k, g)
         for j in range(PACK):
-            load_token_tile(0, j)
+            load_tokens(0, j, 1)
         for g in range(PASSES):
             load_weight_pass(wv_raw, w_v, g)
-        for w in range(1, WINDOWS):
-            for j in range(PACK):
-                load_token_tile(w, j)
+        for j in range(0, PACK, HALF):
+            load_tokens(1, j, HALF)
+        for w in range(2, WINDOWS):
+            load_tokens(w, 0, PACK)
 
         ident = const.tile([P, P], F32, name="ident")
         make_identity(nc, ident[:])
@@ -237,6 +237,8 @@ def tile_localcontextprocessor_pa_t_kernel(tc, x, w_k, w_v, out):
 
             kf[w] = token_operand("kf")
             k_accs, e_tiles = [], []
+            if last:
+                quantise_heads(v[w - 1], 0, HEADS)
             for h in range(HEADS):
                 acc = project(x_q[w], wk_q, h)
                 e = exps.tile([P, 1, DH, PACK], BF16, name="e")
@@ -261,14 +263,19 @@ def tile_localcontextprocessor_pa_t_kernel(tc, x, w_k, w_v, out):
                     transpose_tile(x_q[1], 1, j, False)
                 quantise_window(x_q[1])
 
-            if w > 0:
+            if w > 0 and not last:
                 quantise_heads(v[w - 1], 0, HEADS)
             quantise_heads(kf[w], 0, HEADS)
 
             v[w] = token_operand("v")
             for h in range(HEADS):
+                if last and h == HALF:
+                    c_acc = context_heads(w - 1, kf[w - 1], v[w - 1], 0, HEADS)
+                    store_context(w - 1, c_acc, 0, HEADS, on_scalar=True)
                 acc = project(x_q[w], wv_q, h)
                 nc.scalar.copy(out=head_view(v[w], h), in_=by_column(acc))
+                if last and h == HALF:
+                    quantise_heads(v[w], 0, HALF)
 
             run = RUNS.get(w, ())
             for ahead in run:
@@ -280,11 +287,11 @@ def tile_localcontextprocessor_pa_t_kernel(tc, x, w_k, w_v, out):
             waiting += run[1:]
 
         w = WINDOWS - 1
-        c_before = context_heads(w - 1, kf[w - 1], v[w - 1], 0, HEADS)
-        quantise_heads(v[w], 0, HALF)
-        for h in range(HALF, HEADS):
-            quantise_heads(v[w], h, 1)
-        store_context(w - 1, c_before, 0, HEADS, on_scalar=True)
-        for first in range(0, HEADS, HALF):
-            c_acc = context_heads(w, kf[w], v[w], first, HALF)
-            store_context(w, c_acc, first, HALF, on_scalar=(first > 0))
+        quantise_heads(v[w], HALF, 1)
+        c_acc = context_heads(w, kf[w], v[w], 0, HALF)
+        store_context(w, c_acc, 0, HALF, on_scalar=True)
+        c_acc = context_heads(w, kf[w], v[w], HALF, 1)
+        quantise_heads(v[w], HALF + 1, 1)
+        store_context(w, c_acc, HALF, 1, on_scalar=True)
+        c_acc = context_heads(w, kf[w], v[w], HALF + 1, 1)
+        store_context(w, c_acc, HALF + 1, 1)

from contextlib import ExitStack

import concourse.mybir as mybir
from concourse.masks import make_identity

F32 = mybir.dt.float32
BF16 = mybir.dt.bfloat16
U32 = mybir.dt.uint32
U8 = mybir.dt.uint8
FP8X4 = mybir.dt.float8_e4m3fn_x4
ACT = mybir.ActivationFunctionType
ALU = mybir.AluOpType

P = 128
PACK = 4
K_PASS = P * PACK
WINDOWS = 8
TOKENS = 512
FEATURES = 1024
PASSES = FEATURES // K_PASS
HEADS = 4
DH = 128
INNER = HEADS * DH
PAIRS = 2
HALF = 2
RUNS = {0: (2, 3), 2: (4, 5, 6, 7)}
RUN = 4

FLOPS = 2 * WINDOWS * TOKENS * FEATURES * 2 * INNER + 2 * WINDOWS * HEADS * TOKENS * DH * DH


def tile_localcontextprocessor_pa_t_kernel(tc, x, w_k, w_v, out):
    nc = tc.nc
    with ExitStack() as ctx:
        ctx.enter_context(tc.manual_schedule())
        const = ctx.enter_context(tc.tile_pool(name="const", bufs=1))
        rows = ctx.enter_context(tc.tile_pool(name="rows", bufs=WINDOWS))
        windows = ctx.enter_context(tc.tile_pool(name="windows", bufs=5))
        stage = ctx.enter_context(tc.tile_pool(name="stage", bufs=3))
        outs = ctx.enter_context(tc.tile_pool(name="outs", bufs=4))
        exps = ctx.enter_context(tc.tile_pool(name="exps", bufs=4))
        psum = ctx.enter_context(tc.psum_pool(name="psum", bufs=8))

        x_windows = x.rearrange("b (n p j) d -> (b n) p (j d)", n=2, p=P, j=PACK)
        x_tiles = [
            rows.tile([P, PACK * FEATURES], BF16, name="x_rows") for w in range(WINDOWS)
        ]

        def load_tokens(w, j, count):
            cols = slice(j * FEATURES, (j + count) * FEATURES)
            nc.sync.dma_start(out=x_tiles[w][:, cols], in_=x_windows[w, :, cols])

        wk_raw = const.tile([P, PASSES * PACK * INNER], BF16, name="wk_raw")
        wv_raw = const.tile([P, PASSES * PACK * INNER], BF16, name="wv_raw")

        def load_weight_pass(w_raw, w_dram, g):
            nc.sync.dma_start(
                out=w_raw[:, g * PACK * INNER : (g + 1) * PACK * INNER].rearrange(
                    "q (u r) -> q u r", u=PAIRS
                ),
                in_=w_dram[g * K_PASS : (g + 1) * K_PASS, :].rearrange(
                    "(u q e) c -> q u (e c)", u=PAIRS, q=P, e=2
                ),
            )

        for g in range(PASSES):
            load_weight_pass(wk_raw, w_k, g)
        for j in range(PACK):
            load_tokens(0, j, 1)
        for g in range(PASSES):
            load_weight_pass(wv_raw, w_v, g)
        for j in range(0, PACK, HALF):
            load_tokens(1, j, HALF)
        for w in range(2, WINDOWS):
            load_tokens(w, 0, PACK)

        ident = const.tile([P, P], F32, name="ident")
        make_identity(nc, ident[:])

        warm = const.tile([P, 1], F32, name="warm")
        nc.vector.memset(warm[:], 0.0)
        nc.scalar.activation(out=warm[:], in_=warm[:], func=ACT.Exp)

        def weight_operand(name):
            grp = const.tile([P, PASSES * INNER * PACK], BF16, name=name + "_grp", align_bytes=64)
            codes = const.tile([P, PASSES * INNER], U32, name=name + "_codes", align_bytes=64)
            scales = const.tile([P, PASSES * INNER], U8, name=name + "_scales", align_bytes=64)
            return grp, codes, scales

        def regroup_weight(w_q, w_raw, g, scalar_heads):
            src = w_raw[:].rearrange(
                "q (g t h c i) -> q g h c t i", g=PASSES, t=PACK, h=HEADS, i=RUN
            )
            dst = w_q[0][:].rearrange(
                "q (g h c i t) -> q g h c t i", h=HEADS, g=PASSES, i=RUN, t=PACK
            )
            for h in range(HEADS):
                if h in scalar_heads:
                    nc.scalar.copy(out=dst[:, g, h], in_=src[:, g, h])
                else:
                    nc.vector.tensor_copy(out=dst[:, g, h], in_=src[:, g, h])

        def quantise(operand, first, count):
            grp, codes, scales = operand
            nc.vector.quantize_mx(
                out=codes[:, first : first + count].bitcast(FP8X4),
                scales=scales[:, first : first + count],
                in_=grp[:, first * PACK : (first + count) * PACK],
            )

        def window_operand():
            x_grp = windows.tile([P, TOKENS * PASSES * PACK], BF16, name="x_grp", align_bytes=64)
            x_codes = windows.tile([P, TOKENS * PASSES], U32, name="x_codes", align_bytes=64)
            x_scales = windows.tile([P, TOKENS * PASSES], U8, name="x_scales", align_bytes=64)
            return x_grp, x_codes, x_scales

        def transpose_tile(x_q, w, j, on_vector):
            words = x_tiles[w][:].bitcast(F32)
            x_grp_words = x_q[0][:].bitcast(F32).rearrange(
                "q (j g m u) -> q j g m u", j=PACK, g=PASSES, u=PAIRS
            )
            xt = psum.tile([P, PASSES * PAIRS, P], F32, name="xt", tag="bank")
            for b in range(PASSES * PAIRS):
                first = (j * PASSES * PAIRS + b) * P
                nc.tensor.transpose(
                    out=xt[:, b, :], in_=words[:, first : first + P], identity=ident[:]
                )
            x_words = xt[:].rearrange("q (g u) m -> q g m u", u=PAIRS)
            if on_vector:
                nc.vector.tensor_copy(out=x_grp_words[:, j], in_=x_words)
            else:
                nc.scalar.copy(out=x_grp_words[:, j], in_=x_words)

        def quantise_tiles(x_q, j, count):
            quantise(x_q, j * PASSES * P, count * PASSES * P)

        def quantise_window(x_q):
            for j in range(0, PACK, HALF):
                quantise_tiles(x_q, j, HALF)

        def project_tile(acc, x_q, w_q, h, j):
            for g in range(PASSES):
                tok = slice((j * PASSES + g) * P, (j * PASSES + g + 1) * P)
                col = slice((g * HEADS + h) * DH, (g * HEADS + h + 1) * DH)
                nc.tensor.matmul_mx(
                    out=acc[:, j, :],
                    lhsT=x_q[1][:, tok].bitcast(FP8X4),
                    lhsT_scale=x_q[2][:, tok],
                    rhs=w_q[1][:, col].bitcast(FP8X4),
                    rhs_scale=w_q[2][:, col],
                    start=(g == 0),
                    stop=(g == PASSES - 1),
                )

        def new_bank():
            return psum.tile([P, PACK, DH], F32, name="acc", tag="bank")

        def project(x_q, w_q, h):
            acc = new_bank()
            for j in range(PACK):
                project_tile(acc, x_q, w_q, h, j)
            return acc

        def token_operand(name):
            grp = stage.tile([P, INNER * PACK], BF16, name=name + "_grp", align_bytes=64)
            codes = stage.tile([P, INNER], U32, name=name + "_codes", align_bytes=64)
            scales = stage.tile([P, INNER], U8, name=name + "_scales", align_bytes=64)
            return grp, codes, scales

        def by_column(acc):
            return acc[:].rearrange("p j d -> p d j")

        def head_view(operand, h):
            return operand[0][:].rearrange("p (h d j) -> p h d j", h=HEADS, j=PACK)[:, h]

        def quantise_heads(operand, h, count):
            quantise(operand, h * DH, count * DH)

        def exp_head(e, i, acc):
            nc.scalar.activation(out=e[:, i], in_=by_column(acc), func=ACT.Exp)

        def add_head(kf, h, acc, e, i):
            nc.vector.scalar_tensor_tensor(
                out=head_view(kf, h), in0=by_column(acc), scalar=0.0, in1=e[:, i],
                op0=ALU.max, op1=ALU.add,
            )

        def clip(e):
            nc.vector.tensor_scalar_min(out=e[:], in0=e[:], scalar1=1.0)

        def context_heads(w, kf, v, first, count):
            c_acc = psum.tile([P, count, DH], F32, name="c_acc", tag="bank")
            for i in range(count):
                col = slice((first + i) * DH, (first + i + 1) * DH)
                nc.tensor.matmul_mx(
                    out=c_acc[:, i, :],
                    lhsT=kf[1][:, col].bitcast(FP8X4),
                    lhsT_scale=kf[2][:, col],
                    rhs=v[1][:, col].bitcast(FP8X4),
                    rhs_scale=v[2][:, col],
                    start=True,
                    stop=True,
                )
            return c_acc

        def store_context(w, c_acc, first, count, on_scalar=False):
            c_sb = outs.tile([P, count, DH], F32, name="c_sb")
            if on_scalar:
                nc.scalar.copy(out=c_sb[:], in_=c_acc[:])
            else:
                nc.vector.tensor_copy(out=c_sb[:], in_=c_acc[:])
            nc.sync.dma_start(
                out=out[w, first : first + count].rearrange("h d e -> d h e"), in_=c_sb[:]
            )

        wk_q = weight_operand("wk")
        wv_q = weight_operand("wv")
        x_q = {0: window_operand()}
        kf, v = {}, {}
        waiting = []
        for g in range(PASSES):
            regroup_weight(wk_q, wk_raw, g, (1, 3))
        for j in range(PACK):
            transpose_tile(x_q[0], 0, j, False)
        for g in range(PASSES):
            for h in range(0, HEADS, HALF):
                quantise(wk_q, (g * HEADS + h) * DH, HALF * DH)
        for j in range(PACK):
            quantise_tiles(x_q[0], j, 1)
        for g in range(PASSES):
            regroup_weight(wv_q, wv_raw, g, (1, 3))
        for g in range(PASSES):
            quantise(wv_q, g * INNER, INNER)

        for w in range(WINDOWS):
            last = w + 1 == WINDOWS

            kf[w] = token_operand("kf")
            k_accs, e_tiles = [], []
            if last:
                quantise_heads(v[w - 1], 0, HEADS)
            for h in range(HEADS):
                acc = project(x_q[w], wk_q, h)
                e = exps.tile([P, 1, DH, PACK], BF16, name="e")
                exp_head(e, 0, acc)
                clip(e)
                k_accs.append(acc)
                e_tiles.append(e)
                if h > 0:
                    add_head(kf[w], h - 1, k_accs[h - 1], e_tiles[h - 1], 0)
            add_head(kf[w], HEADS - 1, k_accs[HEADS - 1], e_tiles[HEADS - 1], 0)

            if w >= 2:
                c_acc = context_heads(w - 2, kf[w - 2], v[w - 2], 0, HEADS)
                store_context(w - 2, c_acc, 0, HEADS, on_scalar=True)

            if waiting:
                quantise_window(x_q[waiting.pop(0)])

            if w == 0:
                x_q[1] = window_operand()
                for j in range(PACK):
                    transpose_tile(x_q[1], 1, j, False)
                quantise_window(x_q[1])

            if w > 0 and not last:
                quantise_heads(v[w - 1], 0, HEADS)
            quantise_heads(kf[w], 0, HEADS)

            v[w] = token_operand("v")
            for h in range(HEADS):
                if last and h == HALF:
                    c_acc = context_heads(w - 1, kf[w - 1], v[w - 1], 0, HEADS)
                    store_context(w - 1, c_acc, 0, HEADS, on_scalar=True)
                acc = project(x_q[w], wv_q, h)
                nc.scalar.copy(out=head_view(v[w], h), in_=by_column(acc))
                if last and h == HALF:
                    quantise_heads(v[w], 0, HALF)

            run = RUNS.get(w, ())
            for ahead in run:
                x_q[ahead] = window_operand()
                for j in range(PACK):
                    transpose_tile(x_q[ahead], ahead, j, j % 2 == 1)
            for ahead in run[:1]:
                quantise_window(x_q[ahead])
            waiting += run[1:]

        w = WINDOWS - 1
        quantise_heads(v[w], HALF, 1)
        c_acc = context_heads(w, kf[w], v[w], 0, HALF)
        store_context(w, c_acc, 0, HALF, on_scalar=True)
        c_acc = context_heads(w, kf[w], v[w], HALF, 1)
        quantise_heads(v[w], HALF + 1, 1)
        store_context(w, c_acc, HALF, 1, on_scalar=True)
        c_acc = context_heads(w, kf[w], v[w], HALF + 1, 1)
        store_context(w, c_acc, HALF + 1, 1)
